import numpy as np
import ml_dtypes


def mxq(x, axis, fmt="e4m3"):
    dtype, down = {"e4m3": (ml_dtypes.float8_e4m3fn, 7), "e5m2": (ml_dtypes.float8_e5m2, 14)}[fmt]
    v = np.moveaxis(np.asarray(x, np.float32).astype(ml_dtypes.bfloat16).astype(np.float64), axis, -1)
    blocks = v.reshape(v.shape[:-1] + (-1, 32))
    amax = np.abs(blocks).max(-1, keepdims=True)
    byte = np.maximum(np.where(amax > 0, np.frexp(amax)[1] - 1 + 127, 0) - down, 1)
    scale = np.exp2(byte - 127.0)
    codes = (blocks / scale).astype(np.float32).astype(dtype).astype(np.float64)
    return np.moveaxis((codes * scale).reshape(v.shape), -1, axis)


WIDE = False


def mx_kscale(k):
    if not WIDE:
        return np.ones(k)
    levels = np.array([10, -10, 5, -5, 0])
    if k % 512:
        return np.exp2(np.random.permutation(np.resize(levels, k // 32))).repeat(32)
    a = np.empty((k // 512, 16))
    for p in range(k // 512):
        a[p, :8] = np.random.permutation(np.resize(levels, 8))
        for g in range(8):
            far = levels[np.abs(levels - a[p, g]) >= 10]
            a[p, g + 8] = far[np.random.randint(len(far))]
    return np.exp2(a.ravel()).repeat(32)


BF16 = ml_dtypes.bfloat16


def bf(x):
    return np.asarray(x, np.float32).astype(BF16)


def f64(x):
    return np.asarray(x).astype(np.float64)


B, U, I, O = 1024, 4, 1024, 256


def sigmoid(v):
    return 1.0 / (1.0 + np.exp(-v))


def setup_inputs():
    s = mx_kscale(I)
    wi = lambda: bf(np.random.standard_normal((U, I, O)) / np.sqrt(I) / s[None, :, None])
    wh = lambda: bf(np.random.standard_normal((U, O, O)) / np.sqrt(O))
    return {"x": bf(np.random.standard_normal((B, U, I)) * s),
            "h": bf(np.random.standard_normal((B, U, O))),
            "w_ir": wi(), "w_iz": wi(), "w_in": wi(),
            "w_hr": wh(), "w_hz": wh(), "w_hn": wh()}


def reference(x, h, w_ir, w_iz, w_in, w_hr, w_hz, w_hn):
    xq = mxq(f64(x).transpose(1, 0, 2), 2, "e4m3")
    hu = f64(h).transpose(1, 0, 2)
    r = sigmoid((xq @ mxq(f64(w_ir), 1, "e4m3")) + hu @ f64(w_hr))
    z = sigmoid((xq @ mxq(f64(w_iz), 1, "e4m3")) + hu @ f64(w_hz))
    n = np.tanh((xq @ mxq(f64(w_in), 1, "e4m3")) + r * (hu @ f64(w_hn)))
    return ((1.0 - z) * n + z * hu).transpose(1, 0, 2)

@@ -1,0 +1,325 @@
+from contextlib import ExitStack
+
+import concourse.mybir as mybir
+from concourse.masks import make_identity
+
+F32 = mybir.dt.float32
+BF16 = mybir.dt.bfloat16
+U32 = mybir.dt.uint32
+U8 = mybir.dt.uint8
+FP8X4 = mybir.dt.float8_e4m3fn_x4
+ACT = mybir.ActivationFunctionType
+ALU = mybir.AluOpType
+
+B, U, I, O = 1024, 4, 1024, 256
+GATES = 3
+P = 128
+PACK = 4
+K_PASS = P * PACK
+PASSES = I // K_PASS
+H_TILES = O // P
+PAIR = 2
+STEPS_PER_UNIT = B // (P * PAIR)
+STEPS = U * STEPS_PER_UNIT
+WORDS = I // 2
+HALF = O // 2
+PIECES_PER_GATE = PASSES * (O // HALF)
+PIECES = GATES * PIECES_PER_GATE
+PIECES_PER_STEP = PIECES // STEPS_PER_UNIT
+X_LEAD = 2
+BLEND_LAG = 2
+RZ_COLS = slice(0, 2 * O)
+N_COLS = slice(2 * O, 3 * O)
+
+FLOPS = 2 * B * U * (I + O) * GATES * O
+
+
+def tile_unitwisegru_pa_t_kernel(tc, x, h, w_ir, w_iz, w_in, w_hr, w_hz, w_hn, out):
+    nc = tc.nc
+    input_weights = (w_ir, w_iz, w_in)
+    hidden_weights = (w_hr, w_hz, w_hn)
+
+    with ExitStack() as stack:
+
+        def sbuf_pool(name, bufs):
+            return stack.enter_context(tc.tile_pool(name=name, bufs=bufs))
+
+        const = sbuf_pool("const", 1)
+        w_raw_pool = sbuf_pool("w_raw", 2)
+        w_grouped_pool = sbuf_pool("w_grouped", 2 * PIECES_PER_GATE)
+        w_mx_pool = sbuf_pool("w_mx", 2)
+        w_hidden_pool = sbuf_pool("w_hidden", 3)
+        x_raw_pool = sbuf_pool("x_raw", 4)
+        x_grouped_pool = sbuf_pool("x_grouped", 3)
+        x_mx_pool = sbuf_pool("x_mx", 4)
+        h_rows_pool = sbuf_pool("h_rows", 8)
+        h_cols_pool = sbuf_pool("h_cols", 4)
+        short = sbuf_pool("short", 4)
+        long = sbuf_pool("long", 5)
+        banks = stack.enter_context(tc.psum_pool(name="banks", bufs=8))
+        stack.enter_context(tc.manual_schedule())
+
+        ident_f32 = const.tile([P, P], F32)
+        make_identity(nc, ident_f32[:])
+        ident_bf16 = const.tile([P, P], BF16)
+        make_identity(nc, ident_bf16[:])
+
+        w_raw, w_grouped, w_codes, w_scales, w_hidden = {}, {}, {}, {}, {}
+        x_raw, x_grouped, x_codes, x_scales, h_rows, h_cols = {}, {}, {}, {}, {}, {}
+        hidden_rz_sb, input_rz, rz, hidden_n, input_n = {}, {}, {}, {}, {}
+        gated, sum_n, n, diff, scaled, result = {}, {}, {}, {}, {}, {}
+
+        def live(k):
+            return 0 <= k < STEPS
+
+        def unit_of(k):
+            return k // STEPS_PER_UNIT
+
+        def batch_rows(k):
+            j = k % STEPS_PER_UNIT
+            return slice(j * PAIR * P, (j + 1) * PAIR * P)
+
+
+        def load_input_weight(u, gate):
+            raw = w_raw_pool.tile([P, PASSES, PACK, O], BF16, name="w_raw_%d" % gate)
+            nc.sync.dma_start(
+                out=raw[:].rearrange("p g t o -> p g (t o)"),
+                in_=input_weights[gate][u].rearrange("(g p t) o -> p g (t o)", p=P, t=PACK),
+            )
+            w_raw[(u, gate)] = raw
+
+        def load_hidden_weights(u):
+            w_hidden[u] = w_hidden_pool.tile([P, H_TILES, GATES * O], BF16, name="w_hidden")
+            for gate in range(GATES):
+                nc.sync.dma_start(
+                    out=w_hidden[u][:, :, gate * O : (gate + 1) * O],
+                    in_=hidden_weights[gate][u].rearrange("(k p) o -> p k o", p=P),
+                )
+
+        def load_weights_ahead(s):
+            u, j = divmod(s + 2 * STEPS_PER_UNIT - 1, STEPS_PER_UNIT)
+            if 1 <= u < U:
+                if j < GATES:
+                    load_input_weight(u, j)
+                else:
+                    load_hidden_weights(u)
+
+        def load_step(k):
+            if not live(k):
+                return
+            x_raw[k] = x_raw_pool.tile([P, PAIR, I], BF16, name="x_raw")
+            nc.sync.dma_start(
+                out=x_raw[k][:], in_=x[batch_rows(k), unit_of(k), :].rearrange("(t p) i -> p t i", p=P)
+            )
+            h_rows[k] = h_rows_pool.tile([P, PAIR, O], BF16, name="h_rows")
+            nc.sync.dma_start(
+                out=h_rows[k][:], in_=h[batch_rows(k), unit_of(k), :].rearrange("(t p) o -> p t o", p=P)
+            )
+
+
+        def pieces_regrouped_in(s):
+            if s < 0:
+                first = (s + GATES) * PIECES_PER_GATE
+                return [(0, q) for q in range(max(first, 0), first + PIECES_PER_GATE)]
+            first = PIECES + s * PIECES_PER_STEP
+            return [divmod(i, PIECES) for i in range(first, min(first + PIECES_PER_STEP, U * PIECES))]
+
+        def place_of(q):
+            gate, rest = divmod(q, PIECES_PER_GATE)
+            g, half = divmod(rest, O // HALF)
+            return gate, g, half * HALF
+
+        def regroup_weights(s):
+            for u, q in pieces_regrouped_in(s):
+                gate, g, first = place_of(q)
+                w_grouped[(u, q)] = w_grouped_pool.tile([P, HALF, PACK], BF16, name="w_grouped", align_bytes=64)
+                grouped = w_grouped[(u, q)][:].rearrange("p (c i) t -> p c t i", i=4)
+                rows = w_raw[(u, gate)][:, g, :, first : first + HALF].rearrange("p t (c i) -> p c t i", i=4)
+                if u == 0:
+                    nc.vector.tensor_copy(out=grouped, in_=rows)
+                else:
+                    nc.scalar.copy(out=grouped, in_=rows)
+
+        def quantise_weights(s):
+            for u, q in pieces_regrouped_in(s - 1):
+                gate, g, first = place_of(q)
+                cols = slice(gate * O + first, gate * O + first + HALF)
+                if q == 0:
+                    w_codes[u] = w_mx_pool.tile([P, PASSES, GATES * O], U32, name="w_codes", align_bytes=64)
+                    w_scales[u] = w_mx_pool.tile([P, PASSES, GATES * O], U8, name="w_scales", align_bytes=64)
+                nc.vector.quantize_mx(
+                    out=w_codes[u][:, g, cols].bitcast(FP8X4),
+                    scales=w_scales[u][:, g, cols],
+                    in_=w_grouped[(u, q)][:].rearrange("p o t -> p (o t)"),
+                )
+
+
+        def transpose_x(k):
+            if not live(k):
+                return
+            x_grouped[k] = x_grouped_pool.tile([P, PAIR * I], BF16, name="x_grouped", align_bytes=64)
+            grouped_words = x_grouped[k][:].bitcast(F32)
+            for t in range(PAIR):
+                raw_words = x_raw[k][:, t, :].bitcast(F32)
+                turned = banks.tile([P, WORDS // P, P], F32, name="x_turned", tag="bank")
+                for c in range(WORDS // P):
+                    g, v = divmod(c, 2)
+                    every_second = slice(2 * P * g + v, 2 * P * (g + 1), 2)
+                    nc.tensor.transpose(turned[:, c, :], raw_words[:, every_second], ident_f32[:])
+                grouped = grouped_words[:, t * WORDS : (t + 1) * WORDS].rearrange(
+                    "p (g b v) -> p g b v", g=PASSES, v=2
+                )
+                if k < X_LEAD:
+                    nc.scalar.copy(out=grouped, in_=turned[:].rearrange("p (g v) b -> p g b v", v=2))
+                else:
+                    nc.vector.tensor_copy(out=grouped, in_=turned[:].rearrange("p (g v) b -> p g b v", v=2))
+
+        def quantise_x(k):
+            if not live(k):
+                return
+            x_codes[k] = x_mx_pool.tile([P, PAIR * PASSES * P], U32, name="x_codes", align_bytes=64)
+            x_scales[k] = x_mx_pool.tile([P, PAIR * PASSES * P], U8, name="x_scales", align_bytes=64)
+            nc.vector.quantize_mx(out=x_codes[k][:].bitcast(FP8X4), scales=x_scales[k][:], in_=x_grouped[k][:])
+
+        def transpose_h(k):
+            if not live(k):
+                return
+            turned = banks.tile([P, PAIR, H_TILES, P], BF16, name="h_turned", tag="bank")
+            for t in range(PAIR):
+                for c in range(H_TILES):
+                    nc.tensor.transpose(turned[:, t, c, :], h_rows[k][:, t, c * P : (c + 1) * P], ident_bf16[:])
+            h_cols[k] = h_cols_pool.tile([P, PAIR, H_TILES, P], BF16, name="h_cols")
+            nc.scalar.copy(out=h_cols[k][:], in_=turned[:])
+
+
+        def plain_product(acc, k, t, cols):
+            for c in range(H_TILES):
+                nc.tensor.matmul(
+                    acc,
+                    lhsT=h_cols[k][:, t, c, :],
+                    rhs=w_hidden[unit_of(k)][:, c, cols],
+                    start=(c == 0),
+                    stop=(c == H_TILES - 1),
+                )
+
+        def mx_product(acc, k, t, cols):
+            u = unit_of(k)
+            for g in range(PASSES):
+                batch = slice((t * PASSES + g) * P, (t * PASSES + g + 1) * P)
+                nc.tensor.matmul_mx(
+                    out=acc,
+                    lhsT=x_codes[k][:, batch].bitcast(FP8X4),
+                    lhsT_scale=x_scales[k][:, batch],
+                    rhs=w_codes[u][:, g, cols].bitcast(FP8X4),
+                    rhs_scale=w_scales[u][:, g, cols],
+                    start=(g == 0),
+                    stop=(g == PASSES - 1),
+                )
+
+        def hidden_rz_product(k, t):
+            if not live(k):
+                return
+            acc = banks.tile([P, 2 * O], F32, name="hidden_rz", tag="bank")
+            plain_product(acc[:], k, t, RZ_COLS)
+            hidden_rz_sb[(k, t)] = short.tile([P, 2 * O], F32, name="hidden_rz_sb")
+            nc.scalar.copy(out=hidden_rz_sb[(k, t)][:], in_=acc[:])
+
+        def input_rz_product(k, t):
+            if not live(k):
+                return
+            input_rz[(k, t)] = banks.tile([P, 2 * O], F32, name="input_rz", tag="bank")
+            mx_product(input_rz[(k, t)][:], k, t, RZ_COLS)
+
+        def n_products(k):
+            if not live(k):
+                return
+            input_n[k] = banks.tile([P, PAIR, O], F32, name="input_n", tag="bank")
+            for t in range(PAIR):
+                mx_product(input_n[k][:, t, :], k, t, N_COLS)
+            hidden_n[k] = banks.tile([P, PAIR, O], F32, name="hidden_n", tag="bank")
+            for t in range(PAIR):
+                plain_product(hidden_n[k][:, t, :], k, t, N_COLS)
+
+
+        def sigmoid_rz(k, t):
+            if not live(k):
+                return
+            if t == 0:
+                rz[k] = long.tile([P, PAIR, 2 * O], F32, name="rz")
+            sum_rz = short.tile([P, 2 * O], F32, name="sum_rz")
+            nc.vector.tensor_tensor(out=sum_rz[:], in0=input_rz[(k, t)][:], in1=hidden_rz_sb[(k, t)][:], op=ALU.add)
+            nc.scalar.activation(out=rz[k][:, t, :], in_=sum_rz[:], func=ACT.Sigmoid)
+
+        def gate_hidden_n(k):
+            if not live(k):
+                return
+            gated[k] = short.tile([P, PAIR, O], F32, name="gated")
+            nc.vector.tensor_tensor(out=gated[k][:], in0=hidden_n[k][:], in1=rz[k][:, :, 0:O], op=ALU.mult)
+
+        def add_input_n(k):
+            if not live(k):
+                return
+            sum_n[k] = short.tile([P, PAIR, O], F32, name="sum_n")
+            nc.vector.tensor_tensor(out=sum_n[k][:], in0=input_n[k][:], in1=gated[k][:], op=ALU.add)
+
+        def tanh_n(k):
+            if not live(k):
+                return
+            n[k] = long.tile([P, PAIR, O], F32, name="n")
+            nc.scalar.activation(out=n[k][:], in_=sum_n[k][:], func=ACT.Tanh)
+
+
+        def blend_engine(k):
+            return nc.vector if k + BLEND_LAG >= STEPS else nc.gpsimd
+
+        def blend_difference(k):
+            if not live(k):
+                return
+            diff[k] = short.tile([P, PAIR, O], F32, name="diff")
+            blend_engine(k).tensor_tensor(out=diff[k][:], in0=h_rows[k][:], in1=n[k][:], op=ALU.subtract)
+
+        def blend_scale(k):
+            if not live(k):
+                return
+            scaled[k] = short.tile([P, PAIR, O], F32, name="scaled")
+            blend_engine(k).tensor_tensor(out=scaled[k][:], in0=rz[k][:, :, O : 2 * O], in1=diff[k][:], op=ALU.mult)
+
+        def blend_sum_and_store(k):
+            if not live(k):
+                return
+            result[k] = short.tile([P, PAIR, O], F32, name="result")
+            blend_engine(k).tensor_tensor(out=result[k][:], in0=n[k][:], in1=scaled[k][:], op=ALU.add)
+            nc.sync.dma_start(
+                out=out[batch_rows(k), unit_of(k), :].rearrange("(t p) o -> p t o", p=P), in_=result[k][:]
+            )
+
+
+        load_input_weight(0, 0)
+        load_step(0)
+        load_input_weight(0, 1)
+        load_hidden_weights(0)
+        load_step(1)
+        load_input_weight(0, 2)
+
+        for s in range(-GATES, STEPS + BLEND_LAG + 1):
+            load_weights_ahead(s)
+            load_step(s + 5)
+
+            hidden_rz_product(s, 0)
+            transpose_h(s + 1)
+            hidden_rz_product(s, 1)
+            add_input_n(s - 2)
+            tanh_n(s - 2)
+            quantise_x(s + 1)
+            quantise_weights(s)
+            regroup_weights(s)
+            input_rz_product(s, 0)
+            input_rz_product(s, 1)
+            sigmoid_rz(s, 0)
+            sigmoid_rz(s, 1)
+            n_products(s - 1)
+            gate_hidden_n(s - 1)
+            transpose_x(s + X_LEAD)
+            blend_difference(s - BLEND_LAG)
+            blend_sum_and_store(s - BLEND_LAG - 1)
+            blend_scale(s - BLEND_LAG)

@@ -189,7 +189,7 @@ def tile_unitwisegru_pa_t_kernel(tc, x, h, w_ir, w_iz, w_in, w_hr, w_hz, w_hn, o
                 for c in range(H_TILES):
                     nc.tensor.transpose(turned[:, t, c, :], h_rows[k][:, t, c * P : (c + 1) * P], ident_bf16[:])
             h_cols[k] = h_cols_pool.tile([P, PAIR, H_TILES, P], BF16, name="h_cols")
-            nc.scalar.copy(out=h_cols[k][:], in_=turned[:])
+            nc.vector.tensor_copy(out=h_cols[k][:], in_=turned[:])
 
 
         def plain_product(acc, k, t, cols):

@@ -250,48 +250,58 @@ def tile_unitwisegru_pa_t_kernel(tc, x, h, w_ir, w_iz, w_in, w_hr, w_hz, w_hn, o
             nc.vector.tensor_tensor(out=sum_rz[:], in0=input_rz[(k, t)][:], in1=hidden_rz_sb[(k, t)][:], op=ALU.add)
             nc.scalar.activation(out=rz[k][:, t, :], in_=sum_rz[:], func=ACT.Sigmoid)
 
+        def parts(k):
+            if k < STEPS - 1:
+                return [slice(0, PAIR)]
+            return [slice(t, t + 1) for t in range(PAIR)]
+
         def gate_hidden_n(k):
             if not live(k):
                 return
             gated[k] = short.tile([P, PAIR, O], F32, name="gated")
-            nc.vector.tensor_tensor(out=gated[k][:], in0=hidden_n[k][:], in1=rz[k][:, :, 0:O], op=ALU.mult)
+            for ts in parts(k):
+                nc.vector.tensor_tensor(out=gated[k][:, ts, :], in0=hidden_n[k][:, ts, :], in1=rz[k][:, ts, 0:O], op=ALU.mult)
 
         def add_input_n(k):
             if not live(k):
                 return
             sum_n[k] = short.tile([P, PAIR, O], F32, name="sum_n")
-            nc.vector.tensor_tensor(out=sum_n[k][:], in0=input_n[k][:], in1=gated[k][:], op=ALU.add)
+            for ts in parts(k):
+                nc.vector.tensor_tensor(out=sum_n[k][:, ts, :], in0=input_n[k][:, ts, :], in1=gated[k][:, ts, :], op=ALU.add)
 
         def tanh_n(k):
             if not live(k):
                 return
             n[k] = long.tile([P, PAIR, O], F32, name="n")
-            nc.scalar.activation(out=n[k][:], in_=sum_n[k][:], func=ACT.Tanh)
+            for ts in parts(k):
+                nc.scalar.activation(out=n[k][:, ts, :], in_=sum_n[k][:, ts, :], func=ACT.Tanh)
 
 
-        def blend_engine(k):
-            return nc.vector if k + BLEND_LAG >= STEPS else nc.gpsimd
+        def blend_engine(k, op):
+            return nc.vector if k + 2 >= STEPS or (op == 2 and k + 3 == STEPS) else nc.gpsimd
 
         def blend_difference(k):
             if not live(k):
                 return
             diff[k] = short.tile([P, PAIR, O], F32, name="diff")
-            blend_engine(k).tensor_tensor(out=diff[k][:], in0=h_rows[k][:], in1=n[k][:], op=ALU.subtract)
+            for ts in parts(k):
+                blend_engine(k, 0).tensor_tensor(out=diff[k][:, ts, :], in0=h_rows[k][:, ts, :], in1=n[k][:, ts, :], op=ALU.subtract)
 
         def blend_scale(k):
             if not live(k):
                 return
             scaled[k] = short.tile([P, PAIR, O], F32, name="scaled")
-            blend_engine(k).tensor_tensor(out=scaled[k][:], in0=rz[k][:, :, O : 2 * O], in1=diff[k][:], op=ALU.mult)
+            for ts in parts(k):
+                blend_engine(k, 1).tensor_tensor(out=scaled[k][:, ts, :], in0=rz[k][:, ts, O : 2 * O], in1=diff[k][:, ts, :], op=ALU.mult)
 
         def blend_sum_and_store(k):
             if not live(k):
                 return
             result[k] = short.tile([P, PAIR, O], F32, name="result")
-            blend_engine(k).tensor_tensor(out=result[k][:], in0=n[k][:], in1=scaled[k][:], op=ALU.add)
-            nc.sync.dma_start(
-                out=out[batch_rows(k), unit_of(k), :].rearrange("(t p) o -> p t o", p=P), in_=result[k][:]
-            )
+            rows = out[batch_rows(k), unit_of(k), :].rearrange("(t p) o -> p t o", p=P)
+            for ts in parts(k):
+                blend_engine(k, 2).tensor_tensor(out=result[k][:, ts, :], in0=n[k][:, ts, :], in1=scaled[k][:, ts, :], op=ALU.add)
+                nc.sync.dma_start(out=rows[:, ts, :], in_=result[k][:, ts, :])
 
 
         load_input_weight(0, 0)
@@ -301,7 +311,7 @@ def tile_unitwisegru_pa_t_kernel(tc, x, h, w_ir, w_iz, w_in, w_hr, w_hz, w_hn, o
         load_step(1)
         load_input_weight(0, 2)
 
-        for s in range(-GATES, STEPS + BLEND_LAG + 1):
+        for s in range(-GATES, STEPS):
             load_weights_ahead(s)
             load_step(s + 5)
 
@@ -323,3 +333,17 @@ def tile_unitwisegru_pa_t_kernel(tc, x, h, w_ir, w_iz, w_in, w_hr, w_hz, w_hn, o
             blend_difference(s - BLEND_LAG)
             blend_sum_and_store(s - BLEND_LAG - 1)
             blend_scale(s - BLEND_LAG)
+
+        n_products(STEPS - 1)
+        add_input_n(STEPS - 2)
+        tanh_n(STEPS - 2)
+        gate_hidden_n(STEPS - 1)
+        add_input_n(STEPS - 1)
+        tanh_n(STEPS - 1)
+        blend_difference(STEPS - 2)
+        blend_sum_and_store(STEPS - 3)
+        blend_difference(STEPS - 1)
+        blend_scale(STEPS - 2)
+        blend_scale(STEPS - 1)
+        blend_sum_and_store(STEPS - 2)
+        blend_sum_and_store(STEPS - 1)

@@ -26,8 +26,12 @@ HALF = O // 2
 PIECES_PER_GATE = PASSES * (O // HALF)
 PIECES = GATES * PIECES_PER_GATE
 PIECES_PER_STEP = PIECES // STEPS_PER_UNIT
+LOAD_LEAD = 5
 X_LEAD = 2
 BLEND_LAG = 2
+VECTOR_BLENDS_FROM = STEPS - 2
+VECTOR_ADDS_FROM = STEPS - 3
+COPY_RUN = 4
 RZ_COLS = slice(0, 2 * O)
 N_COLS = slice(2 * O, 3 * O)
 
@@ -133,8 +137,8 @@ def tile_unitwisegru_pa_t_kernel(tc, x, h, w_ir, w_iz, w_in, w_hr, w_hz, w_hn, o
             for u, q in pieces_regrouped_in(s):
                 gate, g, first = place_of(q)
                 w_grouped[(u, q)] = w_grouped_pool.tile([P, HALF, PACK], BF16, name="w_grouped", align_bytes=64)
-                grouped = w_grouped[(u, q)][:].rearrange("p (c i) t -> p c t i", i=4)
-                rows = w_raw[(u, gate)][:, g, :, first : first + HALF].rearrange("p t (c i) -> p c t i", i=4)
+                grouped = w_grouped[(u, q)][:].rearrange("p (c i) t -> p c t i", i=COPY_RUN)
+                rows = w_raw[(u, gate)][:, g, :, first : first + HALF].rearrange("p t (c i) -> p c t i", i=COPY_RUN)
                 if u == 0:
                     nc.vector.tensor_copy(out=grouped, in_=rows)
                 else:
@@ -277,43 +281,46 @@ def tile_unitwisegru_pa_t_kernel(tc, x, h, w_ir, w_iz, w_in, w_hr, w_hz, w_hn, o
                 nc.scalar.activation(out=n[k][:, ts, :], in_=sum_n[k][:, ts, :], func=ACT.Tanh)
 
 
-        def blend_engine(k, op):
-            return nc.vector if k + 2 >= STEPS or (op == 2 and k + 3 == STEPS) else nc.gpsimd
+        def blend_engine(k, vector_from):
+            return nc.vector if k >= vector_from else nc.gpsimd
 
         def blend_difference(k):
             if not live(k):
                 return
             diff[k] = short.tile([P, PAIR, O], F32, name="diff")
+            engine = blend_engine(k, VECTOR_BLENDS_FROM)
             for ts in parts(k):
-                blend_engine(k, 0).tensor_tensor(out=diff[k][:, ts, :], in0=h_rows[k][:, ts, :], in1=n[k][:, ts, :], op=ALU.subtract)
+                engine.tensor_tensor(out=diff[k][:, ts, :], in0=h_rows[k][:, ts, :], in1=n[k][:, ts, :], op=ALU.subtract)
 
         def blend_scale(k):
             if not live(k):
                 return
             scaled[k] = short.tile([P, PAIR, O], F32, name="scaled")
+            engine = blend_engine(k, VECTOR_BLENDS_FROM)
             for ts in parts(k):
-                blend_engine(k, 1).tensor_tensor(out=scaled[k][:, ts, :], in0=rz[k][:, ts, O : 2 * O], in1=diff[k][:, ts, :], op=ALU.mult)
+                engine.tensor_tensor(out=scaled[k][:, ts, :], in0=rz[k][:, ts, O : 2 * O], in1=diff[k][:, ts, :], op=ALU.mult)
 
         def blend_sum_and_store(k):
             if not live(k):
                 return
             result[k] = short.tile([P, PAIR, O], F32, name="result")
             rows = out[batch_rows(k), unit_of(k), :].rearrange("(t p) o -> p t o", p=P)
+            engine = blend_engine(k, VECTOR_ADDS_FROM)
             for ts in parts(k):
-                blend_engine(k, 2).tensor_tensor(out=result[k][:, ts, :], in0=n[k][:, ts, :], in1=scaled[k][:, ts, :], op=ALU.add)
+                engine.tensor_tensor(out=result[k][:, ts, :], in0=n[k][:, ts, :], in1=scaled[k][:, ts, :], op=ALU.add)
                 nc.sync.dma_start(out=rows[:, ts, :], in_=result[k][:, ts, :])
 
 
         load_input_weight(0, 0)
         load_step(0)
         load_input_weight(0, 1)
-        load_hidden_weights(0)
         load_step(1)
+        load_hidden_weights(0)
         load_input_weight(0, 2)
 
         for s in range(-GATES, STEPS):
             load_weights_ahead(s)
-            load_step(s + 5)
+            load_step(s + LOAD_LEAD)
 
             hidden_rz_product(s, 0)
             transpose_h(s + 1)

from contextlib import ExitStack

import concourse.mybir as mybir
from concourse.masks import make_identity

F32 = mybir.dt.float32
BF16 = mybir.dt.bfloat16
U32 = mybir.dt.uint32
U8 = mybir.dt.uint8
FP8X4 = mybir.dt.float8_e4m3fn_x4
ACT = mybir.ActivationFunctionType
ALU = mybir.AluOpType

B, U, I, O = 1024, 4, 1024, 256
GATES = 3
P = 128
PACK = 4
K_PASS = P * PACK
PASSES = I // K_PASS
H_TILES = O // P
PAIR = 2
STEPS_PER_UNIT = B // (P * PAIR)
STEPS = U * STEPS_PER_UNIT
WORDS = I // 2
HALF = O // 2
PIECES_PER_GATE = PASSES * (O // HALF)
PIECES = GATES * PIECES_PER_GATE
PIECES_PER_STEP = PIECES // STEPS_PER_UNIT
LOAD_LEAD = 5
X_LEAD = 2
BLEND_LAG = 2
VECTOR_BLENDS_FROM = STEPS - 2
VECTOR_ADDS_FROM = STEPS - 3
COPY_RUN = 4
RZ_COLS = slice(0, 2 * O)
N_COLS = slice(2 * O, 3 * O)

FLOPS = 2 * B * U * (I + O) * GATES * O


def tile_unitwisegru_pa_t_kernel(tc, x, h, w_ir, w_iz, w_in, w_hr, w_hz, w_hn, out):
    nc = tc.nc
    input_weights = (w_ir, w_iz, w_in)
    hidden_weights = (w_hr, w_hz, w_hn)

    with ExitStack() as stack:

        def sbuf_pool(name, bufs):
            return stack.enter_context(tc.tile_pool(name=name, bufs=bufs))

        const = sbuf_pool("const", 1)
        w_raw_pool = sbuf_pool("w_raw", 2)
        w_grouped_pool = sbuf_pool("w_grouped", 2 * PIECES_PER_GATE)
        w_mx_pool = sbuf_pool("w_mx", 2)
        w_hidden_pool = sbuf_pool("w_hidden", 3)
        x_raw_pool = sbuf_pool("x_raw", 4)
        x_grouped_pool = sbuf_pool("x_grouped", 3)
        x_mx_pool = sbuf_pool("x_mx", 4)
        h_rows_pool = sbuf_pool("h_rows", 8)
        h_cols_pool = sbuf_pool("h_cols", 4)
        short = sbuf_pool("short", 4)
        long = sbuf_pool("long", 5)
        banks = stack.enter_context(tc.psum_pool(name="banks", bufs=8))
        stack.enter_context(tc.manual_schedule())

        ident_f32 = const.tile([P, P], F32)
        make_identity(nc, ident_f32[:])
        ident_bf16 = const.tile([P, P], BF16)
        make_identity(nc, ident_bf16[:])

        w_raw, w_grouped, w_codes, w_scales, w_hidden = {}, {}, {}, {}, {}
        x_raw, x_grouped, x_codes, x_scales, h_rows, h_cols = {}, {}, {}, {}, {}, {}
        hidden_rz_sb, input_rz, rz, hidden_n, input_n = {}, {}, {}, {}, {}
        gated, sum_n, n, diff, scaled, result = {}, {}, {}, {}, {}, {}

        def live(k):
            return 0 <= k < STEPS

        def unit_of(k):
            return k // STEPS_PER_UNIT

        def batch_rows(k):
            j = k % STEPS_PER_UNIT
            return slice(j * PAIR * P, (j + 1) * PAIR * P)


        def load_input_weight(u, gate):
            raw = w_raw_pool.tile([P, PASSES, PACK, O], BF16, name="w_raw_%d" % gate)
            nc.sync.dma_start(
                out=raw[:].rearrange("p g t o -> p g (t o)"),
                in_=input_weights[gate][u].rearrange("(g p t) o -> p g (t o)", p=P, t=PACK),
            )
            w_raw[(u, gate)] = raw

        def load_hidden_weights(u):
            w_hidden[u] = w_hidden_pool.tile([P, H_TILES, GATES * O], BF16, name="w_hidden")
            for gate in range(GATES):
                nc.sync.dma_start(
                    out=w_hidden[u][:, :, gate * O : (gate + 1) * O],
                    in_=hidden_weights[gate][u].rearrange("(k p) o -> p k o", p=P),
                )

        def load_weights_ahead(s):
            u, j = divmod(s + 2 * STEPS_PER_UNIT - 1, STEPS_PER_UNIT)
            if 1 <= u < U:
                if j < GATES:
                    load_input_weight(u, j)
                else:
                    load_hidden_weights(u)

        def load_step(k):
            if not live(k):
                return
            x_raw[k] = x_raw_pool.tile([P, PAIR, I], BF16, name="x_raw")
            nc.sync.dma_start(
                out=x_raw[k][:], in_=x[batch_rows(k), unit_of(k), :].rearrange("(t p) i -> p t i", p=P)
            )
            h_rows[k] = h_rows_pool.tile([P, PAIR, O], BF16, name="h_rows")
            nc.sync.dma_start(
                out=h_rows[k][:], in_=h[batch_rows(k), unit_of(k), :].rearrange("(t p) o -> p t o", p=P)
            )


        def pieces_regrouped_in(s):
            if s < 0:
                first = (s + GATES) * PIECES_PER_GATE
                return [(0, q) for q in range(max(first, 0), first + PIECES_PER_GATE)]
            first = PIECES + s * PIECES_PER_STEP
            return [divmod(i, PIECES) for i in range(first, min(first + PIECES_PER_STEP, U * PIECES))]

        def place_of(q):
            gate, rest = divmod(q, PIECES_PER_GATE)
            g, half = divmod(rest, O // HALF)
            return gate, g, half * HALF

        def regroup_weights(s):
            for u, q in pieces_regrouped_in(s):
                gate, g, first = place_of(q)
                w_grouped[(u, q)] = w_grouped_pool.tile([P, HALF, PACK], BF16, name="w_grouped", align_bytes=64)
                grouped = w_grouped[(u, q)][:].rearrange("p (c i) t -> p c t i", i=COPY_RUN)
                rows = w_raw[(u, gate)][:, g, :, first : first + HALF].rearrange("p t (c i) -> p c t i", i=COPY_RUN)
                if u == 0:
                    nc.vector.tensor_copy(out=grouped, in_=rows)
                else:
                    nc.scalar.copy(out=grouped, in_=rows)

        def quantise_weights(s):
            for u, q in pieces_regrouped_in(s - 1):
                gate, g, first = place_of(q)
                cols = slice(gate * O + first, gate * O + first + HALF)
                if q == 0:
                    w_codes[u] = w_mx_pool.tile([P, PASSES, GATES * O], U32, name="w_codes", align_bytes=64)
                    w_scales[u] = w_mx_pool.tile([P, PASSES, GATES * O], U8, name="w_scales", align_bytes=64)
                nc.vector.quantize_mx(
                    out=w_codes[u][:, g, cols].bitcast(FP8X4),
                    scales=w_scales[u][:, g, cols],
                    in_=w_grouped[(u, q)][:].rearrange("p o t -> p (o t)"),
                )


        def transpose_x(k):
            if not live(k):
                return
            x_grouped[k] = x_grouped_pool.tile([P, PAIR * I], BF16, name="x_grouped", align_bytes=64)
            grouped_words = x_grouped[k][:].bitcast(F32)
            for t in range(PAIR):
                raw_words = x_raw[k][:, t, :].bitcast(F32)
                turned = banks.tile([P, WORDS // P, P], F32, name="x_turned", tag="bank")
                for c in range(WORDS // P):
                    g, v = divmod(c, 2)
                    every_second = slice(2 * P * g + v, 2 * P * (g + 1), 2)
                    nc.tensor.transpose(turned[:, c, :], raw_words[:, every_second], ident_f32[:])
                grouped = grouped_words[:, t * WORDS : (t + 1) * WORDS].rearrange(
                    "p (g b v) -> p g b v", g=PASSES, v=2
                )
                if k < X_LEAD:
                    nc.scalar.copy(out=grouped, in_=turned[:].rearrange("p (g v) b -> p g b v", v=2))
                else:
                    nc.vector.tensor_copy(out=grouped, in_=turned[:].rearrange("p (g v) b -> p g b v", v=2))

        def quantise_x(k):
            if not live(k):
                return
            x_codes[k] = x_mx_pool.tile([P, PAIR * PASSES * P], U32, name="x_codes", align_bytes=64)
            x_scales[k] = x_mx_pool.tile([P, PAIR * PASSES * P], U8, name="x_scales", align_bytes=64)
            nc.vector.quantize_mx(out=x_codes[k][:].bitcast(FP8X4), scales=x_scales[k][:], in_=x_grouped[k][:])

        def transpose_h(k):
            if not live(k):
                return
            turned = banks.tile([P, PAIR, H_TILES, P], BF16, name="h_turned", tag="bank")
            for t in range(PAIR):
                for c in range(H_TILES):
                    nc.tensor.transpose(turned[:, t, c, :], h_rows[k][:, t, c * P : (c + 1) * P], ident_bf16[:])
            h_cols[k] = h_cols_pool.tile([P, PAIR, H_TILES, P], BF16, name="h_cols")
            nc.vector.tensor_copy(out=h_cols[k][:], in_=turned[:])


        def plain_product(acc, k, t, cols):
            for c in range(H_TILES):
                nc.tensor.matmul(
                    acc,
                    lhsT=h_cols[k][:, t, c, :],
                    rhs=w_hidden[unit_of(k)][:, c, cols],
                    start=(c == 0),
                    stop=(c == H_TILES - 1),
                )

        def mx_product(acc, k, t, cols):
            u = unit_of(k)
            for g in range(PASSES):
                batch = slice((t * PASSES + g) * P, (t * PASSES + g + 1) * P)
                nc.tensor.matmul_mx(
                    out=acc,
                    lhsT=x_codes[k][:, batch].bitcast(FP8X4),
                    lhsT_scale=x_scales[k][:, batch],
                    rhs=w_codes[u][:, g, cols].bitcast(FP8X4),
                    rhs_scale=w_scales[u][:, g, cols],
                    start=(g == 0),
                    stop=(g == PASSES - 1),
                )

        def hidden_rz_product(k, t):
            if not live(k):
                return
            acc = banks.tile([P, 2 * O], F32, name="hidden_rz", tag="bank")
            plain_product(acc[:], k, t, RZ_COLS)
            hidden_rz_sb[(k, t)] = short.tile([P, 2 * O], F32, name="hidden_rz_sb")
            nc.scalar.copy(out=hidden_rz_sb[(k, t)][:], in_=acc[:])

        def input_rz_product(k, t):
            if not live(k):
                return
            input_rz[(k, t)] = banks.tile([P, 2 * O], F32, name="input_rz", tag="bank")
            mx_product(input_rz[(k, t)][:], k, t, RZ_COLS)

        def n_products(k):
            if not live(k):
                return
            input_n[k] = banks.tile([P, PAIR, O], F32, name="input_n", tag="bank")
            for t in range(PAIR):
                mx_product(input_n[k][:, t, :], k, t, N_COLS)
            hidden_n[k] = banks.tile([P, PAIR, O], F32, name="hidden_n", tag="bank")
            for t in range(PAIR):
                plain_product(hidden_n[k][:, t, :], k, t, N_COLS)


        def sigmoid_rz(k, t):
            if not live(k):
                return
            if t == 0:
                rz[k] = long.tile([P, PAIR, 2 * O], F32, name="rz")
            sum_rz = short.tile([P, 2 * O], F32, name="sum_rz")
            nc.vector.tensor_tensor(out=sum_rz[:], in0=input_rz[(k, t)][:], in1=hidden_rz_sb[(k, t)][:], op=ALU.add)
            nc.scalar.activation(out=rz[k][:, t, :], in_=sum_rz[:], func=ACT.Sigmoid)

        def parts(k):
            if k < STEPS - 1:
                return [slice(0, PAIR)]
            return [slice(t, t + 1) for t in range(PAIR)]

        def gate_hidden_n(k):
            if not live(k):
                return
            gated[k] = short.tile([P, PAIR, O], F32, name="gated")
            for ts in parts(k):
                nc.vector.tensor_tensor(out=gated[k][:, ts, :], in0=hidden_n[k][:, ts, :], in1=rz[k][:, ts, 0:O], op=ALU.mult)

        def add_input_n(k):
            if not live(k):
                return
            sum_n[k] = short.tile([P, PAIR, O], F32, name="sum_n")
            for ts in parts(k):
                nc.vector.tensor_tensor(out=sum_n[k][:, ts, :], in0=input_n[k][:, ts, :], in1=gated[k][:, ts, :], op=ALU.add)

        def tanh_n(k):
            if not live(k):
                return
            n[k] = long.tile([P, PAIR, O], F32, name="n")
            for ts in parts(k):
                nc.scalar.activation(out=n[k][:, ts, :], in_=sum_n[k][:, ts, :], func=ACT.Tanh)


        def blend_engine(k, vector_from):
            return nc.vector if k >= vector_from else nc.gpsimd

        def blend_difference(k):
            if not live(k):
                return
            diff[k] = short.tile([P, PAIR, O], F32, name="diff")
            engine = blend_engine(k, VECTOR_BLENDS_FROM)
            for ts in parts(k):
                engine.tensor_tensor(out=diff[k][:, ts, :], in0=h_rows[k][:, ts, :], in1=n[k][:, ts, :], op=ALU.subtract)

        def blend_scale(k):
            if not live(k):
                return
            scaled[k] = short.tile([P, PAIR, O], F32, name="scaled")
            engine = blend_engine(k, VECTOR_BLENDS_FROM)
            for ts in parts(k):
                engine.tensor_tensor(out=scaled[k][:, ts, :], in0=rz[k][:, ts, O : 2 * O], in1=diff[k][:, ts, :], op=ALU.mult)

        def blend_sum_and_store(k):
            if not live(k):
                return
            result[k] = short.tile([P, PAIR, O], F32, name="result")
            rows = out[batch_rows(k), unit_of(k), :].rearrange("(t p) o -> p t o", p=P)
            engine = blend_engine(k, VECTOR_ADDS_FROM)
            for ts in parts(k):
                engine.tensor_tensor(out=result[k][:, ts, :], in0=n[k][:, ts, :], in1=scaled[k][:, ts, :], op=ALU.add)
                nc.sync.dma_start(out=rows[:, ts, :], in_=result[k][:, ts, :])


        load_input_weight(0, 0)
        load_step(0)
        load_input_weight(0, 1)
        load_step(1)
        load_hidden_weights(0)
        load_input_weight(0, 2)

        for s in range(-GATES, STEPS):
            load_weights_ahead(s)
            load_step(s + LOAD_LEAD)

            hidden_rz_product(s, 0)
            transpose_h(s + 1)
            hidden_rz_product(s, 1)
            add_input_n(s - 2)
            tanh_n(s - 2)
            quantise_x(s + 1)
            quantise_weights(s)
            regroup_weights(s)
            input_rz_product(s, 0)
            input_rz_product(s, 1)
            sigmoid_rz(s, 0)
            sigmoid_rz(s, 1)
            n_products(s - 1)
            gate_hidden_n(s - 1)
            transpose_x(s + X_LEAD)
            blend_difference(s - BLEND_LAG)
            blend_sum_and_store(s - BLEND_LAG - 1)
            blend_scale(s - BLEND_LAG)

        n_products(STEPS - 1)
        add_input_n(STEPS - 2)
        tanh_n(STEPS - 2)
        gate_hidden_n(STEPS - 1)
        add_input_n(STEPS - 1)
        tanh_n(STEPS - 1)
        blend_difference(STEPS - 2)
        blend_sum_and_store(STEPS - 3)
        blend_difference(STEPS - 1)
        blend_scale(STEPS - 2)
        blend_scale(STEPS - 1)
        blend_sum_and_store(STEPS - 2)
        blend_sum_and_store(STEPS - 1)
